import numpy as np
import ml_dtypes


def mxq(x, axis, fmt="e4m3"):
    dtype, down = {"e4m3": (ml_dtypes.float8_e4m3fn, 7), "e5m2": (ml_dtypes.float8_e5m2, 14)}[fmt]
    v = np.moveaxis(np.asarray(x, np.float32).astype(ml_dtypes.bfloat16).astype(np.float64), axis, -1)
    blocks = v.reshape(v.shape[:-1] + (-1, 32))
    amax = np.abs(blocks).max(-1, keepdims=True)
    byte = np.maximum(np.where(amax > 0, np.frexp(amax)[1] - 1 + 127, 0) - down, 1)
    scale = np.exp2(byte - 127.0)
    codes = (blocks / scale).astype(np.float32).astype(dtype).astype(np.float64)
    return np.moveaxis((codes * scale).reshape(v.shape), -1, axis)


WIDE = False


def mx_kscale(k):
    if not WIDE:
        return np.ones(k)
    levels = np.array([30, -30])
    if k % 512:
        return np.exp2(np.random.permutation(np.resize(levels, k // 32))).repeat(32)
    a = np.empty((k // 512, 16))
    for p in range(k // 512):
        a[p, :8] = np.random.permutation(np.resize(levels, 8))
        for g in range(8):
            far = levels[np.abs(levels - a[p, g]) >= 10]
            a[p, g + 8] = far[np.random.randint(len(far))]
    return np.exp2(a.ravel()).repeat(32)


BF16 = ml_dtypes.bfloat16


def bf(x):
    return np.asarray(x, np.float32).astype(BF16)


def f64(x):
    return np.asarray(x).astype(np.float64)


B, CIN, H, W, CP, G = 3, 2048, 16, 16, 1024, 2
CG = CP // G
CO = CIN // G
HW = H * W
EPS = 1e-5


def setup_inputs():
    s = mx_kscale(CG)
    return {"y": bf((np.random.standard_normal((B, G, CG, HW)) * 2.5 + 1.0) * s[None, None, :, None]),
            "Wz": bf((np.random.standard_normal((G, CO, CG)) / np.sqrt(CG) + 1.5 / CG) / s),
            "gamma": bf(1.0 + 0.1 * np.random.standard_normal(CIN)),
            "beta": bf(0.1 * np.random.standard_normal(CIN)),
            "x": bf(np.random.standard_normal((B, CIN, H, W)))}


def reference(y, Wz, gamma, beta, x):
    z = mxq(f64(Wz), 2, "e5m2") @ mxq(f64(y), 2, "e4m3")
    zr = z.reshape(B, G, CO * HW)
    mu = zr.mean(-1, keepdims=True)
    var = zr.var(-1, keepdims=True)
    zn = ((zr - mu) * (1.0 / np.sqrt(var + EPS))).reshape(B, CIN, H, W)
    return zn * f64(gamma)[None, :, None, None] + f64(beta)[None, :, None, None] + f64(x)

@@ -1,0 +1,352 @@
+from contextlib import ExitStack
+
+import concourse.mybir as mybir
+from concourse.masks import make_identity
+
+B, G, CG, CO, HW = 3, 2, 512, 1024, 256
+EPS = 1e-5
+FLOPS = 2 * B * G * CO * CG * HW
+
+F32 = mybir.dt.float32
+BF16 = mybir.dt.bfloat16
+U32 = mybir.dt.uint32
+U8 = mybir.dt.uint8
+E4M3X4 = mybir.dt.float8_e4m3fn_x4
+E5M2X4 = mybir.dt.float8_e5m2_x4
+ALU = mybir.AluOpType
+ACT = mybir.ActivationFunctionType
+
+P = 128
+PACK = 4
+TILES = CO // P
+PAIRS = TILES // 2
+UNITS = B * G
+KEPT_BANKS = ((0, 1), (2, 3))
+STAT_BANK = 4
+AGAIN_BANK = 5
+COUNT = CO * HW
+STAT_W = 8
+ADD_COL = 64
+
+
+def tile_spatialcgnl_pb_kernel(tc, y, Wz, gamma, beta, x, out):
+    nc = tc.nc
+    with ExitStack() as ctx:
+        sb = ctx.enter_context(tc.tile_pool(name="sb", bufs=1))
+        psum = ctx.enter_context(tc.psum_pool(name="psum", bufs=1))
+        ctx.enter_context(tc.manual_schedule())
+
+        w_hbm = Wz.rearrange("j (p t) k -> j p t k", t=TILES)
+        y_hbm = y.rearrange("b j (p i) w -> b j p (i w)", i=PACK)
+        x_hbm = x.rearrange("b (j p t) h w -> b j p (t h w)", j=G, t=TILES)
+        out_hbm = out.rearrange("b (j p t) h w -> b j p (t h w)", j=G, t=TILES)
+
+        ident = sb.tile([P, P], F32)
+        average = sb.tile([P, P], F32)
+        gamma_raw = sb.tile([P, G, TILES], BF16)
+        beta_raw = sb.tile([P, G, TILES], BF16)
+        addends = sb.tile([P, G, 2, TILES], F32)
+        factors = sb.tile([P, G, 1 + B, TILES], F32)
+        w_raw = sb.tile([P, G, TILES, CG], BF16, align_bytes=64)
+        w_grouped = sb.tile([P, G, PAIRS, 2 * P * PACK], BF16, align_bytes=64)
+        w_codes = sb.tile([P, G, CO], U32, align_bytes=64)
+        w_scales = sb.tile([P, G, CO], U8, align_bytes=64)
+        y_raw = sb.tile([P, UNITS, PACK * HW], BF16, align_bytes=64)
+        y_grouped = sb.tile([P, UNITS, HW * PACK], BF16, align_bytes=64)
+        y_codes = sb.tile([P, UNITS, HW], U32, align_bytes=64)
+        y_scales = sb.tile([P, UNITS, HW], U8, align_bytes=64)
+        x_sb = sb.tile([P, UNITS, TILES * HW], BF16, align_bytes=64)
+        o_sb = sb.tile([P, UNITS, TILES * HW], F32, align_bytes=64)
+        squares = sb.tile([P, 2, 2 * HW], BF16, align_bytes=64)
+        sums = sb.tile([P, UNITS, STAT_W], F32)
+        terms = sb.tile([P, UNITS, STAT_W], F32)
+        neg_mean = sb.tile([P, STAT_W], F32)
+        mean_sq = sb.tile([P, STAT_W], F32)
+        neg_variance = sb.tile([P, UNITS, STAT_W], F32)
+        std = sb.tile([P, UNITS, STAT_W], F32)
+        rstd = sb.tile([P, UNITS, STAT_W], F32)
+        affine = sb.tile([P, UNITS, 2, TILES], F32)
+        small = psum.tile([P, 2 * HW], F32, name="small", tag="small")
+        total = psum.tile([P, 2 * HW], F32, name="total", tag="total")
+        z_banks = {}
+        t_banks = {}
+
+        def group_of(u):
+            return u // B
+
+        def image_of(u):
+            return u % B
+
+        def bank(slot, name):
+            return psum.tile([P, 2 * HW], F32, name=name, tag="bank%d" % slot)
+
+        def load_w(j, q0, q1):
+            nc.sync.dma_start(out=w_raw[:, j, 2 * q0 : 2 * q1, :], in_=w_hbm[j, :, 2 * q0 : 2 * q1, :])
+
+        def load_y(u):
+            nc.sync.dma_start(out=y_raw[:, u, :], in_=y_hbm[image_of(u), group_of(u)])
+
+        def load_x(u):
+            nc.sync.dma_start(out=x_sb[:, u, :], in_=x_hbm[image_of(u), group_of(u)])
+
+        def transpose_w(j, q, slot):
+            tb = bank(slot, "wt_%d_%d" % (j, q))
+            t_banks[j, q] = tb
+            for s in range(2):
+                words = w_raw[:, j, 2 * q + s, :].bitcast(F32)
+                for h in range(2):
+                    col = (2 * s + h) * P
+                    nc.tensor.transpose(tb[:, col : col + P], words[:, h : 2 * P : 2], ident[:])
+
+        def copy_w(j, q, on_vector):
+            dst = w_grouped[:, j, q, :].bitcast(F32).rearrange("p (s r h) -> p s r h", s=2, h=2)
+            src = t_banks[j, q][:].rearrange("p (s h r) -> p s r h", s=2, h=2)
+            if on_vector:
+                nc.vector.tensor_copy(out=dst, in_=src)
+            else:
+                nc.scalar.copy(out=dst, in_=src)
+
+        def quantize_w(j, q):
+            cols = slice(2 * P * q, 2 * P * (q + 1))
+            nc.vector.quantize_mx(out=w_codes[:, j, cols].bitcast(E5M2X4), scales=w_scales[:, j, cols], in_=w_grouped[:, j, q, :])
+
+        def interleave_y(u):
+            nc.vector.tensor_copy(
+                out=y_grouped[:, u, :].rearrange("p (c n i) -> p c i n", n=4, i=PACK),
+                in_=y_raw[:, u, :].rearrange("p (i c n) -> p c i n", n=4, i=PACK),
+            )
+
+        def quantize_y(u):
+            nc.vector.quantize_mx(out=y_codes[:, u, :].bitcast(E4M3X4), scales=y_scales[:, u, :], in_=y_grouped[:, u, :])
+
+        def mx_pass(dst, u, t, cols, start, stop):
+            w_cols = slice(t * P, (t + 1) * P)
+            j = group_of(u)
+            nc.tensor.matmul_mx(
+                out=dst,
+                lhsT=w_codes[:, j, w_cols].bitcast(E5M2X4),
+                lhsT_scale=w_scales[:, j, w_cols],
+                rhs=y_codes[:, u, cols].bitcast(E4M3X4),
+                rhs_scale=y_scales[:, u, cols],
+                start=start,
+                stop=stop,
+            )
+
+        def fill(slot, name, u, q):
+            zb = bank(slot, name)
+            z_banks[u, q] = zb
+            for s in range(2):
+                mx_pass(zb[:, s * HW : (s + 1) * HW], u, 2 * q + s, slice(0, HW), True, True)
+
+        def product(u, q):
+            fill(KEPT_BANKS[u % 2][q // 2] if q % 2 else STAT_BANK, "z_%d_%d" % (u, q), u, q)
+
+        def product_again(u, q):
+            fill(AGAIN_BANK, "zz_%d_%d" % (u, q), u, q)
+
+        def sum_passes(u, t0, t1):
+            for t in range(t0, t1):
+                mx_pass(total[:, 0:HW], u, t, slice(0, HW), t == 0, t == TILES - 1)
+
+        def reduce_sum(u):
+            nc.vector.tensor_reduce(out=sums[:, u, PAIRS : PAIRS + 1], in_=total[:, 0:HW], axis=mybir.AxisListType.X, op=ALU.add)
+
+        def sum_squares(u, q):
+            nc.scalar.activation(out=squares[:, q % 2, :], in_=z_banks[u, q][:], func=ACT.Square, accum_out=sums[:, u, q : q + 1])
+
+        def averages(row, c0, c1):
+            return small[:, STAT_W * row + c0 : STAT_W * row + c1]
+
+        def average_sums(u):
+            nc.tensor.matmul(averages(u, 0, PAIRS + 1), lhsT=average[:], rhs=sums[:, u, 0 : PAIRS + 1], start=True, stop=True)
+
+        def take_mean(u):
+            mean = averages(u, PAIRS, PAIRS + 1)
+            nc.scalar.activation(out=mean_sq[:, u : u + 1], in_=mean, func=ACT.Square, scale=0.5)
+            nc.scalar.activation(out=neg_mean[:, u : u + 1], in_=mean, func=ACT.Copy, scale=-1.0)
+
+        def take_variance(u):
+            nc.scalar.activation(
+                out=terms[:, u, 0:PAIRS], in_=averages(u, 0, PAIRS), func=ACT.Identity,
+                scale=-1.0, bias=mean_sq[:, u : u + 1], accum_out=neg_variance[:, u, 0:1],
+            )
+
+        def take_std(u):
+            nc.scalar.activation(out=std[:, u, 0:1], in_=neg_variance[:, u, 0:1], func=ACT.Sqrt, scale=-1.0, bias=EPS)
+
+        def make_rstd(u):
+            nc.vector.reciprocal(out=rstd[:, u, 0:1], in_=std[:, u, 0:1])
+
+        def make_factors(u):
+            j = group_of(u)
+            nc.scalar.activation(out=factors[:, j, 1 + image_of(u), :], in_=factors[:, j, 0, :], func=ACT.Copy, scale=neg_mean[:, u : u + 1])
+
+        def make_affine(u):
+            j, step = group_of(u), 1 + image_of(u)
+            nc.vector.scalar_tensor_tensor(
+                out=affine[:, u, :, :], in0=factors[:, j, 0 : step + 1 : step, :], scalar=rstd[:, u, 0:1],
+                in1=small[:, ADD_COL + 2 * TILES * j : ADD_COL + 2 * TILES * (j + 1)].rearrange("p (r t) -> p r t", r=2), op0=ALU.mult, op1=ALU.add,
+            )
+
+        def scale_and_add(u, t):
+            cols = slice(t * HW, (t + 1) * HW)
+            s = t % 2
+            nc.vector.scalar_tensor_tensor(
+                out=o_sb[:, u, cols], in0=z_banks[u, t // 2][:, s * HW : (s + 1) * HW], scalar=affine[:, u, 0, t : t + 1],
+                in1=x_sb[:, u, cols], op0=ALU.mult, op1=ALU.add,
+            )
+
+        def add_shift(u, t):
+            cols = slice(t * HW, (t + 1) * HW)
+            nc.gpsimd.tensor_scalar(
+                out=o_sb[:, u, cols], in0=o_sb[:, u, cols], scalar1=1.0, scalar2=affine[:, u, 1, t : t + 1], op0=ALU.mult, op1=ALU.add
+            )
+
+        def place_addends():
+            nc.scalar.activation(out=addends[:, :, 1, :], in_=beta_raw[:], func=ACT.Copy)
+            nc.tensor.matmul(
+                small[:, ADD_COL : ADD_COL + 2 * G * TILES], lhsT=ident[:], rhs=addends[:].rearrange("p j r t -> p (j r t)"), start=True, stop=True
+            )
+
+        def store(u, t0, t1):
+            cols = slice(t0 * HW, t1 * HW)
+            nc.sync.dma_start(out=out_hbm[image_of(u), group_of(u), :, cols], in_=o_sb[:, u, cols])
+
+        nc.scalar.dma_start(out=gamma_raw[:], in_=gamma.rearrange("(j p t) -> p j t", j=G, t=TILES))
+        nc.scalar.dma_start(out=beta_raw[:], in_=beta.rearrange("(j p t) -> p j t", j=G, t=TILES))
+        make_identity(nc, ident[:])
+        nc.gpsimd.memset(average[:], 1.0 / COUNT)
+        nc.gpsimd.memset(addends[:, :, 0, :], 0.0)
+        load_w(0, 0, 1)
+        load_y(0)
+        load_w(0, 1, 2)
+        load_w(0, 2, 3)
+        load_w(0, 3, 4)
+        load_w(1, 0, 2)
+        load_y(1)
+        load_w(1, 2, 4)
+        for u in range(2, UNITS):
+            load_y(u)
+        for u in range(UNITS):
+            load_x(u)
+
+        nc.scalar.activation(out=factors[:, :, 0, :], in_=gamma_raw[:], func=ACT.Copy)
+        transpose_w(0, 0, 2)
+        copy_w(0, 0, False)
+        interleave_y(0)
+        place_addends()
+        transpose_w(0, 1, 3)
+        copy_w(0, 1, False)
+        quantize_w(0, 0)
+        quantize_y(0)
+        transpose_w(0, 2, 5)
+        copy_w(0, 2, True)
+        transpose_w(0, 3, 1)
+        copy_w(0, 3, False)
+        quantize_w(0, 1)
+        quantize_w(0, 2)
+        quantize_w(0, 3)
+        product(0, 0)
+        sum_squares(0, 0)
+        product(0, 1)
+        sum_squares(0, 1)
+        sum_passes(0, 0, 4)
+        transpose_w(1, 0, 2)
+        transpose_w(1, 1, 3)
+        interleave_y(1)
+        copy_w(1, 0, True)
+        quantize_y(1)
+        copy_w(1, 1, True)
+        product(0, 2)
+        sum_squares(0, 2)
+        product(0, 3)
+        sum_squares(0, 3)
+        sum_passes(0, 4, 8)
+        transpose_w(1, 2, 5)
+        transpose_w(1, 3, 2)
+        reduce_sum(0)
+        interleave_y(2)
+        quantize_w(1, 0)
+        quantize_y(2)
+        copy_w(1, 2, False)
+        product(1, 0)
+        average_sums(0)
+        sum_squares(1, 0)
+        take_mean(0)
+        take_variance(0)
+        make_factors(0)
+        take_std(0)
+        copy_w(1, 3, False)
+        sum_passes(1, 0, 4)
+        product(1, 2)
+        sum_squares(1, 2)
+        product(1, 3)
+        sum_squares(1, 3)
+        sum_passes(1, 4, 8)
+        product(1, 1)
+        product_again(0, 0)
+        interleave_y(3)
+        quantize_w(1, 1)
+        quantize_y(3)
+        interleave_y(4)
+        quantize_w(1, 2)
+        quantize_y(4)
+        make_rstd(0)
+        interleave_y(5)
+        make_affine(0)
+        reduce_sum(1)
+        quantize_w(1, 3)
+        quantize_y(5)
+        product(2, 0)
+        sum_passes(2, 0, 3)
+
+        for u in range(UNITS):
+            n1, n2, n3 = u + 1, u + 2, u + 3
+            if n1 < UNITS:
+                sum_squares(n1, 1 if u == 0 else 3)
+            if n2 < UNITS:
+                sum_passes(n2, 3, 7)
+                sum_squares(n2, 0)
+            if n1 < UNITS:
+                average_sums(n1)
+                take_mean(n1)
+                take_variance(n1)
+                make_factors(n1)
+                take_std(n1)
+            scale_and_add(u, 2)
+            scale_and_add(u, 3)
+            add_shift(u, 2)
+            scale_and_add(u, 0)
+            add_shift(u, 3)
+            scale_and_add(u, 1)
+            add_shift(u, 0)
+            if n2 < UNITS:
+                product(n2, 1)
+                sum_passes(n2, 7, 8)
+                product(n2, 2)
+                sum_squares(n2, 2)
+                sum_squares(n2, 1)
+            product_again(u, 2)
+            scale_and_add(u, 6)
+            add_shift(u, 1)
+            store(u, 0, 4)
+            scale_and_add(u, 7)
+            add_shift(u, 6)
+            if n2 < UNITS:
+                reduce_sum(n2)
+                product(n2, 3)
+            if n3 < UNITS:
+                sum_passes(n3, 0, 3)
+                product(n3, 0)
+            if n1 < UNITS:
+                make_rstd(n1)
+            scale_and_add(u, 4)
+            add_shift(u, 7)
+            if n1 < UNITS:
+                make_affine(n1)
+            scale_and_add(u, 5)
+            add_shift(u, 4)
+            add_shift(u, 5)
+            store(u, 4, TILES)
+            if n1 < UNITS:
+                product_again(n1, 0)

@@ -57,7 +57,7 @@ def tile_spatialcgnl_pb_kernel(tc, y, Wz, gamma, beta, x, out):
         y_scales = sb.tile([P, UNITS, HW], U8, align_bytes=64)
         x_sb = sb.tile([P, UNITS, TILES * HW], BF16, align_bytes=64)
         o_sb = sb.tile([P, UNITS, TILES * HW], F32, align_bytes=64)
-        squares = sb.tile([P, 2, 2 * HW], BF16, align_bytes=64)
+        squares = sb.tile([P, PAIRS, 2 * HW], BF16, align_bytes=64)
         sums = sb.tile([P, UNITS, STAT_W], F32)
         terms = sb.tile([P, UNITS, STAT_W], F32)
         neg_mean = sb.tile([P, STAT_W], F32)
@@ -152,7 +152,7 @@ def tile_spatialcgnl_pb_kernel(tc, y, Wz, gamma, beta, x, out):
             nc.vector.tensor_reduce(out=sums[:, u, PAIRS : PAIRS + 1], in_=total[:, 0:HW], axis=mybir.AxisListType.X, op=ALU.add)
 
         def sum_squares(u, q):
-            nc.scalar.activation(out=squares[:, q % 2, :], in_=z_banks[u, q][:], func=ACT.Square, accum_out=sums[:, u, q : q + 1])
+            nc.scalar.activation(out=squares[:, q, :], in_=z_banks[u, q][:], func=ACT.Square, accum_out=sums[:, u, q : q + 1])
 
         def averages(row, c0, c1):
             return small[:, STAT_W * row + c0 : STAT_W * row + c1]
@@ -202,6 +202,14 @@ def tile_spatialcgnl_pb_kernel(tc, y, Wz, gamma, beta, x, out):
                 out=o_sb[:, u, cols], in0=o_sb[:, u, cols], scalar1=1.0, scalar2=affine[:, u, 1, t : t + 1], op0=ALU.mult, op1=ALU.add
             )
 
+        def add_shift_scalar(u, t):
+            cols = slice(t * HW, (t + 1) * HW)
+            nc.scalar.activation(out=o_sb[:, u, cols], in_=o_sb[:, u, cols], func=ACT.Identity, bias=affine[:, u, 1, t : t + 1])
+
+        def add_shift_vector(u, t):
+            cols = slice(t * HW, (t + 1) * HW)
+            nc.vector.tensor_scalar(out=o_sb[:, u, cols], in0=o_sb[:, u, cols], scalar1=affine[:, u, 1, t : t + 1], scalar2=None, op0=ALU.add)
+
         def place_addends():
             nc.scalar.activation(out=addends[:, :, 1, :], in_=beta_raw[:], func=ACT.Copy)
             nc.tensor.matmul(
@@ -217,16 +225,10 @@ def tile_spatialcgnl_pb_kernel(tc, y, Wz, gamma, beta, x, out):
         make_identity(nc, ident[:])
         nc.gpsimd.memset(average[:], 1.0 / COUNT)
         nc.gpsimd.memset(addends[:, :, 0, :], 0.0)
-        load_w(0, 0, 1)
-        load_y(0)
-        load_w(0, 1, 2)
-        load_w(0, 2, 3)
-        load_w(0, 3, 4)
-        load_w(1, 0, 2)
-        load_y(1)
-        load_w(1, 2, 4)
-        for u in range(2, UNITS):
-            load_y(u)
+        for i in range(G * PAIRS):
+            load_w(i // PAIRS, i % PAIRS, i % PAIRS + 1)
+            if i < UNITS:
+                load_y(i)
         for u in range(UNITS):
             load_x(u)
 
@@ -234,119 +236,145 @@ def tile_spatialcgnl_pb_kernel(tc, y, Wz, gamma, beta, x, out):
         transpose_w(0, 0, 2)
         copy_w(0, 0, False)
         interleave_y(0)
-        place_addends()
         transpose_w(0, 1, 3)
+        place_addends()
         copy_w(0, 1, False)
         quantize_w(0, 0)
         quantize_y(0)
+        interleave_y(1)
+        quantize_w(0, 1)
+        quantize_y(1)
         transpose_w(0, 2, 5)
-        copy_w(0, 2, True)
+        copy_w(0, 2, False)
+        product(0, 0)
+        sum_passes(0, 0, 2)
+        sum_squares(0, 0)
         transpose_w(0, 3, 1)
         copy_w(0, 3, False)
-        quantize_w(0, 1)
-        quantize_w(0, 2)
-        quantize_w(0, 3)
-        product(0, 0)
-        sum_squares(0, 0)
-        product(0, 1)
-        sum_squares(0, 1)
-        sum_passes(0, 0, 4)
-        transpose_w(1, 0, 2)
-        transpose_w(1, 1, 3)
-        interleave_y(1)
-        copy_w(1, 0, True)
-        quantize_y(1)
-        copy_w(1, 1, True)
-        product(0, 2)
-        sum_squares(0, 2)
-        product(0, 3)
-        sum_squares(0, 3)
-        sum_passes(0, 4, 8)
-        transpose_w(1, 2, 5)
-        transpose_w(1, 3, 2)
-        reduce_sum(0)
         interleave_y(2)
-        quantize_w(1, 0)
+        quantize_w(0, 2)
         quantize_y(2)
-        copy_w(1, 2, False)
+        product(0, 1)
+        sum_passes(0, 2, 4)
+        sum_squares(0, 1)
+        product(0, 2)
+        sum_passes(0, 4, 6)
+        sum_squares(0, 2)
+        transpose_w(1, 0, 2)
+        interleave_y(3)
+        quantize_w(0, 3)
+        quantize_y(3)
+        product(0, 3)
+        sum_passes(0, 6, 8)
+        copy_w(1, 0, False)
+        sum_squares(0, 3)
+        interleave_y(4)
+        reduce_sum(0)
+        quantize_y(4)
         product(1, 0)
+        transpose_w(1, 1, 3)
         average_sums(0)
         sum_squares(1, 0)
         take_mean(0)
+        copy_w(1, 1, False)
         take_variance(0)
-        make_factors(0)
-        take_std(0)
-        copy_w(1, 3, False)
-        sum_passes(1, 0, 4)
+        transpose_w(1, 2, 2)
+        transpose_w(1, 3, 5)
         product(1, 2)
-        sum_squares(1, 2)
-        product(1, 3)
-        sum_squares(1, 3)
-        sum_passes(1, 4, 8)
-        product(1, 1)
-        product_again(0, 0)
-        interleave_y(3)
-        quantize_w(1, 1)
-        quantize_y(3)
-        interleave_y(4)
-        quantize_w(1, 2)
-        quantize_y(4)
-        make_rstd(0)
         interleave_y(5)
-        make_affine(0)
-        reduce_sum(1)
-        quantize_w(1, 3)
+        quantize_w(1, 0)
         quantize_y(5)
+        copy_w(1, 2, True)
+        copy_w(1, 3, False)
+        take_std(0)
+        make_factors(0)
+        sum_squares(1, 2)
+        sum_passes(1, 0, 4)
+        product(1, 1)
+        sum_squares(1, 1)
+        product(1, 3)
+        product_again(0, 0)
+        sum_passes(1, 4, 8)
+        quantize_w(1, 1)
+        make_rstd(0)
+        quantize_w(1, 2)
+        make_affine(0)
+        quantize_w(1, 3)
         product(2, 0)
-        sum_passes(2, 0, 3)
 
         for u in range(UNITS):
             n1, n2, n3 = u + 1, u + 2, u + 3
-            if n1 < UNITS:
-                sum_squares(n1, 1 if u == 0 else 3)
-            if n2 < UNITS:
-                sum_passes(n2, 3, 7)
-                sum_squares(n2, 0)
-            if n1 < UNITS:
+            last = n1 == UNITS
+            if last:
+                for i, t in enumerate((2, 3, 6, 7, 4, 5, 0, 1)):
+                    scale_and_add(u, t)
+                    if i in (0, 3):
+                        add_shift(u, t)
+                    elif i < 6:
+                        add_shift_scalar(u, t)
+                    if i % 2 and i < 6:
+                        store(u, t - 1, t + 1)
+                for t in (0, 1):
+                    add_shift_vector(u, t)
+                    store(u, t, t + 1)
+                break
+            if u == 0:
+                scale_and_add(u, 0)
+                reduce_sum(1)
+            sum_squares(n1, 3)
+            if u == 0:
                 average_sums(n1)
-                take_mean(n1)
-                take_variance(n1)
-                make_factors(n1)
-                take_std(n1)
-            scale_and_add(u, 2)
-            scale_and_add(u, 3)
-            add_shift(u, 2)
-            scale_and_add(u, 0)
-            add_shift(u, 3)
-            scale_and_add(u, 1)
+            if n2 < UNITS:
+                sum_passes(n2, 0, 5)
+                sum_squares(n2, 0)
+            if u > 0:
+                average_sums(n1)
+            take_mean(n1)
+            if u > 0:
+                scale_and_add(u, 0)
             add_shift(u, 0)
+            scale_and_add(u, 1)
+            add_shift_scalar(u, 1)
+            take_variance(n1)
+            store(u, 0, 2)
+            if n2 < UNITS:
+                sum_passes(n2, 5, 6)
+                product(n2, 2)
+            product_again(u, 2)
+            scale_and_add(u, 2)
+            add_shift(u, 2)
+            scale_and_add(u, 3)
+            add_shift(u, 3)
+            store(u, 2, 4)
+            if n2 < UNITS:
+                sum_squares(n2, 2)
+            take_std(n1)
+            make_factors(n1)
             if n2 < UNITS:
                 product(n2, 1)
-                sum_passes(n2, 7, 8)
-                product(n2, 2)
-                sum_squares(n2, 2)
                 sum_squares(n2, 1)
-            product_again(u, 2)
+                sum_passes(n2, 6, 8)
             scale_and_add(u, 6)
-            add_shift(u, 1)
-            store(u, 0, 4)
-            scale_and_add(u, 7)
             add_shift(u, 6)
+            scale_and_add(u, 7)
             if n2 < UNITS:
-                reduce_sum(n2)
                 product(n2, 3)
             if n3 < UNITS:
-                sum_passes(n3, 0, 3)
                 product(n3, 0)
-            if n1 < UNITS:
-                make_rstd(n1)
             scale_and_add(u, 4)
-            add_shift(u, 7)
-            if n1 < UNITS:
-                make_affine(n1)
             scale_and_add(u, 5)
-            add_shift(u, 4)
-            add_shift(u, 5)
-            store(u, 4, TILES)
-            if n1 < UNITS:
-                product_again(n1, 0)
+            product_again(n1, 0)
+            make_rstd(n1)
+            if n2 < UNITS:
+                reduce_sum(n2)
+                make_affine(n1)
+                for t in (7, 4, 5):
+                    add_shift_vector(u, t)
+                store(u, 4, TILES)
+            else:
+                add_shift_scalar(u, 7)
+                store(u, 6, 8)
+                make_affine(n1)
+                add_shift_scalar(u, 4)
+                add_shift_scalar(u, 5)
+                store(u, 4, 6)

@@ -232,11 +232,19 @@ def tile_spatialcgnl_pb_kernel(tc, y, Wz, gamma, beta, x, out):
         for u in range(UNITS):
             load_x(u)
 
+        ones = sb.tile([P, HW], F32)
+        root = sb.tile([P, STAT_W], F32)
+        nc.vector.memset(ones[:], 1.0)
+        nc.scalar.activation(out=root[:, 0:1], in_=ones[:, 0:1], func=ACT.Sqrt)
         nc.scalar.activation(out=factors[:, :, 0, :], in_=gamma_raw[:], func=ACT.Copy)
+        nc.tensor.matmul(total[:, 0:HW], lhsT=ones[:, 0:P], rhs=ones[:], start=True, stop=True)
+        nc.tensor.matmul(total[:, 0:HW], lhsT=ones[:, 0:P], rhs=ones[:], start=True, stop=True)
         transpose_w(0, 0, 2)
+        nc.tensor.matmul(total[:, 0:HW], lhsT=ones[:, 0:P], rhs=ones[:], start=True, stop=True)
         copy_w(0, 0, False)
         interleave_y(0)
         transpose_w(0, 1, 3)
+        nc.tensor.matmul(total[:, 0:HW], lhsT=ones[:, 0:P], rhs=ones[:], start=True, stop=True)
         place_addends()
         copy_w(0, 1, False)
         quantize_w(0, 0)

@@ -106,18 +106,25 @@ def tile_spatialcgnl_pb_kernel(tc, y, Wz, gamma, beta, x, out):
             else:
                 nc.scalar.copy(out=dst, in_=src)
 
-        def quantize_w(j, q):
-            cols = slice(2 * P * q, 2 * P * (q + 1))
-            nc.vector.quantize_mx(out=w_codes[:, j, cols].bitcast(E5M2X4), scales=w_scales[:, j, cols], in_=w_grouped[:, j, q, :])
-
-        def interleave_y(u):
-            nc.vector.tensor_copy(
-                out=y_grouped[:, u, :].rearrange("p (c n i) -> p c i n", n=4, i=PACK),
-                in_=y_raw[:, u, :].rearrange("p (i c n) -> p c i n", n=4, i=PACK),
+        def quantize_w(j, q0, q1):
+            cols = slice(2 * P * q0, 2 * P * q1)
+            nc.vector.quantize_mx(
+                out=w_codes[:, j, cols].bitcast(E5M2X4), scales=w_scales[:, j, cols],
+                in_=w_grouped[:, j, q0:q1, :].rearrange("p q c -> p (q c)"),
             )
 
-        def quantize_y(u):
-            nc.vector.quantize_mx(out=y_codes[:, u, :].bitcast(E4M3X4), scales=y_scales[:, u, :], in_=y_grouped[:, u, :])
+        def interleave_y(u0, u1):
+            nc.vector.tensor_copy(
+                out=y_grouped[:, u0:u1, :].rearrange("p u (c n i) -> p u c i n", n=4, i=PACK),
+                in_=y_raw[:, u0:u1, :].rearrange("p u (i c n) -> p u c i n", n=4, i=PACK),
+            )
+
+        def quantize_y(u0, u1):
+            nc.vector.quantize_mx(
+                out=y_codes[:, u0:u1, :].rearrange("p u w -> p (u w)").bitcast(E4M3X4),
+                scales=y_scales[:, u0:u1, :].rearrange("p u w -> p (u w)"),
+                in_=y_grouped[:, u0:u1, :].rearrange("p u c -> p (u c)"),
+            )
 
         def mx_pass(dst, u, t, cols, start, stop):
             w_cols = slice(t * P, (t + 1) * P)
@@ -211,7 +218,6 @@ def tile_spatialcgnl_pb_kernel(tc, y, Wz, gamma, beta, x, out):
             nc.vector.tensor_scalar(out=o_sb[:, u, cols], in0=o_sb[:, u, cols], scalar1=affine[:, u, 1, t : t + 1], scalar2=None, op0=ALU.add)
 
         def place_addends():
-            nc.scalar.activation(out=addends[:, :, 1, :], in_=beta_raw[:], func=ACT.Copy)
             nc.tensor.matmul(
                 small[:, ADD_COL : ADD_COL + 2 * G * TILES], lhsT=ident[:], rhs=addends[:].rearrange("p j r t -> p (j r t)"), start=True, stop=True
             )
@@ -220,15 +226,25 @@ def tile_spatialcgnl_pb_kernel(tc, y, Wz, gamma, beta, x, out):
             cols = slice(t0 * HW, t1 * HW)
             nc.sync.dma_start(out=out_hbm[image_of(u), group_of(u), :, cols], in_=o_sb[:, u, cols])
 
-        nc.scalar.dma_start(out=gamma_raw[:], in_=gamma.rearrange("(j p t) -> p j t", j=G, t=TILES))
-        nc.scalar.dma_start(out=beta_raw[:], in_=beta.rearrange("(j p t) -> p j t", j=G, t=TILES))
         make_identity(nc, ident[:])
         nc.gpsimd.memset(average[:], 1.0 / COUNT)
         nc.gpsimd.memset(addends[:, :, 0, :], 0.0)
-        for i in range(G * PAIRS):
-            load_w(i // PAIRS, i % PAIRS, i % PAIRS + 1)
-            if i < UNITS:
-                load_y(i)
+        load_w(0, 0, 1)
+        load_y(0)
+        load_w(0, 1, 2)
+        load_w(0, 2, 3)
+        load_y(1)
+        load_w(0, 3, 4)
+        load_w(1, 0, 1)
+        nc.sync.dma_start(out=gamma_raw[:], in_=gamma.rearrange("(j p t) -> p j t", j=G, t=TILES))
+        nc.sync.dma_start(out=beta_raw[:], in_=beta.rearrange("(j p t) -> p j t", j=G, t=TILES))
+        load_y(2)
+        load_y(3)
+        load_w(1, 1, 2)
+        load_w(1, 2, 3)
+        load_y(4)
+        load_w(1, 3, 4)
+        load_y(5)
         for u in range(UNITS):
             load_x(u)
 
@@ -236,78 +252,74 @@ def tile_spatialcgnl_pb_kernel(tc, y, Wz, gamma, beta, x, out):
         root = sb.tile([P, STAT_W], F32)
         nc.vector.memset(ones[:], 1.0)
         nc.scalar.activation(out=root[:, 0:1], in_=ones[:, 0:1], func=ACT.Sqrt)
-        nc.scalar.activation(out=factors[:, :, 0, :], in_=gamma_raw[:], func=ACT.Copy)
         nc.tensor.matmul(total[:, 0:HW], lhsT=ones[:, 0:P], rhs=ones[:], start=True, stop=True)
         nc.tensor.matmul(total[:, 0:HW], lhsT=ones[:, 0:P], rhs=ones[:], start=True, stop=True)
         transpose_w(0, 0, 2)
         nc.tensor.matmul(total[:, 0:HW], lhsT=ones[:, 0:P], rhs=ones[:], start=True, stop=True)
         copy_w(0, 0, False)
-        interleave_y(0)
+        interleave_y(0, 1)
         transpose_w(0, 1, 3)
-        nc.tensor.matmul(total[:, 0:HW], lhsT=ones[:, 0:P], rhs=ones[:], start=True, stop=True)
-        place_addends()
-        copy_w(0, 1, False)
-        quantize_w(0, 0)
-        quantize_y(0)
-        interleave_y(1)
-        quantize_w(0, 1)
-        quantize_y(1)
         transpose_w(0, 2, 5)
+        nc.tensor.matmul(total[:, 0:HW], lhsT=ones[:, 0:P], rhs=ones[:], start=True, stop=True)
+        copy_w(0, 1, False)
         copy_w(0, 2, False)
+        quantize_w(0, 0, 1)
+        quantize_y(0, 1)
         product(0, 0)
         sum_passes(0, 0, 2)
         sum_squares(0, 0)
+        interleave_y(1, 2)
+        quantize_w(0, 1, 2)
+        quantize_y(1, 2)
+        quantize_w(0, 2, 3)
         transpose_w(0, 3, 1)
+        transpose_w(1, 0, 2)
         copy_w(0, 3, False)
-        interleave_y(2)
-        quantize_w(0, 2)
-        quantize_y(2)
+        nc.scalar.activation(out=factors[:, :, 0, :], in_=gamma_raw[:], func=ACT.Copy)
+        nc.scalar.activation(out=addends[:, :, 1, :], in_=beta_raw[:], func=ACT.Copy)
         product(0, 1)
         sum_passes(0, 2, 4)
         sum_squares(0, 1)
         product(0, 2)
         sum_passes(0, 4, 6)
         sum_squares(0, 2)
-        transpose_w(1, 0, 2)
-        interleave_y(3)
-        quantize_w(0, 3)
-        quantize_y(3)
+        copy_w(1, 0, True)
+        quantize_w(0, 3, 4)
+        quantize_w(1, 0, 1)
+        interleave_y(2, 4)
         product(0, 3)
         sum_passes(0, 6, 8)
-        copy_w(1, 0, False)
         sum_squares(0, 3)
-        interleave_y(4)
         reduce_sum(0)
-        quantize_y(4)
+        quantize_y(2, 4)
         product(1, 0)
         transpose_w(1, 1, 3)
+        place_addends()
         average_sums(0)
         sum_squares(1, 0)
         take_mean(0)
         copy_w(1, 1, False)
         take_variance(0)
-        transpose_w(1, 2, 2)
-        transpose_w(1, 3, 5)
+        make_factors(0)
+        take_std(0)
         product(1, 2)
-        interleave_y(5)
-        quantize_w(1, 0)
-        quantize_y(5)
+        sum_squares(1, 2)
+        sum_passes(1, 0, 3)
+        transpose_w(1, 2, 5)
+        transpose_w(1, 3, 2)
+        interleave_y(4, 6)
         copy_w(1, 2, True)
         copy_w(1, 3, False)
-        take_std(0)
-        make_factors(0)
-        sum_squares(1, 2)
-        sum_passes(1, 0, 4)
-        product(1, 1)
-        sum_squares(1, 1)
         product(1, 3)
+        sum_squares(1, 3)
+        sum_passes(1, 3, 8)
+        product(1, 1)
         product_again(0, 0)
-        sum_passes(1, 4, 8)
-        quantize_w(1, 1)
         make_rstd(0)
-        quantize_w(1, 2)
+        quantize_y(4, 6)
         make_affine(0)
-        quantize_w(1, 3)
+        reduce_sum(1)
+        quantize_w(1, 1, 2)
         product(2, 0)
 
         for u in range(UNITS):
@@ -326,27 +338,20 @@ def tile_spatialcgnl_pb_kernel(tc, y, Wz, gamma, beta, x, out):
                     add_shift_vector(u, t)
                     store(u, t, t + 1)
                 break
-            if u == 0:
-                scale_and_add(u, 0)
-                reduce_sum(1)
-            sum_squares(n1, 3)
-            if u == 0:
-                average_sums(n1)
+            sum_squares(n1, 1 if u == 0 else 3)
             if n2 < UNITS:
-                sum_passes(n2, 0, 5)
+                sum_passes(n2, 0, 3)
                 sum_squares(n2, 0)
-            if u > 0:
-                average_sums(n1)
+            average_sums(n1)
             take_mean(n1)
-            if u > 0:
-                scale_and_add(u, 0)
+            scale_and_add(u, 0)
             add_shift(u, 0)
             scale_and_add(u, 1)
             add_shift_scalar(u, 1)
             take_variance(n1)
             store(u, 0, 2)
             if n2 < UNITS:
-                sum_passes(n2, 5, 6)
+                sum_passes(n2, 3, 6)
                 product(n2, 2)
             product_again(u, 2)
             scale_and_add(u, 2)
@@ -363,20 +368,28 @@ def tile_spatialcgnl_pb_kernel(tc, y, Wz, gamma, beta, x, out):
                 sum_squares(n2, 1)
                 sum_passes(n2, 6, 8)
             scale_and_add(u, 6)
-            add_shift(u, 6)
+            if n2 < UNITS:
+                add_shift(u, 6)
+            else:
+                add_shift_scalar(u, 6)
             scale_and_add(u, 7)
             if n2 < UNITS:
+                add_shift(u, 7)
                 product(n2, 3)
             if n3 < UNITS:
                 product(n3, 0)
             scale_and_add(u, 4)
+            if n2 == UNITS:
+                make_rstd(n1)
             scale_and_add(u, 5)
             product_again(n1, 0)
-            make_rstd(n1)
             if n2 < UNITS:
+                make_rstd(n1)
                 reduce_sum(n2)
                 make_affine(n1)
-                for t in (7, 4, 5):
+                if u == 0:
+                    quantize_w(1, 2, 4)
+                for t in (4, 5):
                     add_shift_vector(u, t)
                 store(u, 4, TILES)
             else:

from contextlib import ExitStack

import concourse.mybir as mybir
from concourse.masks import make_identity

B, G, CG, CO, HW = 3, 2, 512, 1024, 256
EPS = 1e-5
FLOPS = 2 * B * G * CO * CG * HW

F32 = mybir.dt.float32
BF16 = mybir.dt.bfloat16
U32 = mybir.dt.uint32
U8 = mybir.dt.uint8
E4M3X4 = mybir.dt.float8_e4m3fn_x4
E5M2X4 = mybir.dt.float8_e5m2_x4
ALU = mybir.AluOpType
ACT = mybir.ActivationFunctionType

P = 128
PACK = 4
TILES = CO // P
PAIRS = TILES // 2
UNITS = B * G
KEPT_BANKS = ((0, 1), (2, 3))
STAT_BANK = 4
AGAIN_BANK = 5
COUNT = CO * HW
STAT_W = 8
ADD_COL = 64


def tile_spatialcgnl_pb_kernel(tc, y, Wz, gamma, beta, x, out):
    nc = tc.nc
    with ExitStack() as ctx:
        sb = ctx.enter_context(tc.tile_pool(name="sb", bufs=1))
        psum = ctx.enter_context(tc.psum_pool(name="psum", bufs=1))
        ctx.enter_context(tc.manual_schedule())

        w_hbm = Wz.rearrange("j (p t) k -> j p t k", t=TILES)
        y_hbm = y.rearrange("b j (p i) w -> b j p (i w)", i=PACK)
        x_hbm = x.rearrange("b (j p t) h w -> b j p (t h w)", j=G, t=TILES)
        out_hbm = out.rearrange("b (j p t) h w -> b j p (t h w)", j=G, t=TILES)

        ident = sb.tile([P, P], F32)
        average = sb.tile([P, P], F32)
        gamma_raw = sb.tile([P, G, TILES], BF16)
        beta_raw = sb.tile([P, G, TILES], BF16)
        addends = sb.tile([P, G, 2, TILES], F32)
        factors = sb.tile([P, G, 1 + B, TILES], F32)
        w_raw = sb.tile([P, G, TILES, CG], BF16, align_bytes=64)
        w_grouped = sb.tile([P, G, PAIRS, 2 * P * PACK], BF16, align_bytes=64)
        w_codes = sb.tile([P, G, CO], U32, align_bytes=64)
        w_scales = sb.tile([P, G, CO], U8, align_bytes=64)
        y_raw = sb.tile([P, UNITS, PACK * HW], BF16, align_bytes=64)
        y_grouped = sb.tile([P, UNITS, HW * PACK], BF16, align_bytes=64)
        y_codes = sb.tile([P, UNITS, HW], U32, align_bytes=64)
        y_scales = sb.tile([P, UNITS, HW], U8, align_bytes=64)
        x_sb = sb.tile([P, UNITS, TILES * HW], BF16, align_bytes=64)
        o_sb = sb.tile([P, UNITS, TILES * HW], F32, align_bytes=64)
        squares = sb.tile([P, PAIRS, 2 * HW], BF16, align_bytes=64)
        sums = sb.tile([P, UNITS, STAT_W], F32)
        terms = sb.tile([P, UNITS, STAT_W], F32)
        neg_mean = sb.tile([P, STAT_W], F32)
        mean_sq = sb.tile([P, STAT_W], F32)
        neg_variance = sb.tile([P, UNITS, STAT_W], F32)
        std = sb.tile([P, UNITS, STAT_W], F32)
        rstd = sb.tile([P, UNITS, STAT_W], F32)
        affine = sb.tile([P, UNITS, 2, TILES], F32)
        small = psum.tile([P, 2 * HW], F32, name="small", tag="small")
        total = psum.tile([P, 2 * HW], F32, name="total", tag="total")
        z_banks = {}
        t_banks = {}

        def group_of(u):
            return u // B

        def image_of(u):
            return u % B

        def bank(slot, name):
            return psum.tile([P, 2 * HW], F32, name=name, tag="bank%d" % slot)

        def load_w(j, q0, q1):
            nc.sync.dma_start(out=w_raw[:, j, 2 * q0 : 2 * q1, :], in_=w_hbm[j, :, 2 * q0 : 2 * q1, :])

        def load_y(u):
            nc.sync.dma_start(out=y_raw[:, u, :], in_=y_hbm[image_of(u), group_of(u)])

        def load_x(u):
            nc.sync.dma_start(out=x_sb[:, u, :], in_=x_hbm[image_of(u), group_of(u)])

        def transpose_w(j, q, slot):
            tb = bank(slot, "wt_%d_%d" % (j, q))
            t_banks[j, q] = tb
            for s in range(2):
                words = w_raw[:, j, 2 * q + s, :].bitcast(F32)
                for h in range(2):
                    col = (2 * s + h) * P
                    nc.tensor.transpose(tb[:, col : col + P], words[:, h : 2 * P : 2], ident[:])

        def copy_w(j, q, on_vector):
            dst = w_grouped[:, j, q, :].bitcast(F32).rearrange("p (s r h) -> p s r h", s=2, h=2)
            src = t_banks[j, q][:].rearrange("p (s h r) -> p s r h", s=2, h=2)
            if on_vector:
                nc.vector.tensor_copy(out=dst, in_=src)
            else:
                nc.scalar.copy(out=dst, in_=src)

        def quantize_w(j, q0, q1):
            cols = slice(2 * P * q0, 2 * P * q1)
            nc.vector.quantize_mx(
                out=w_codes[:, j, cols].bitcast(E5M2X4), scales=w_scales[:, j, cols],
                in_=w_grouped[:, j, q0:q1, :].rearrange("p q c -> p (q c)"),
            )

        def interleave_y(u0, u1):
            nc.vector.tensor_copy(
                out=y_grouped[:, u0:u1, :].rearrange("p u (c n i) -> p u c i n", n=4, i=PACK),
                in_=y_raw[:, u0:u1, :].rearrange("p u (i c n) -> p u c i n", n=4, i=PACK),
            )

        def quantize_y(u0, u1):
            nc.vector.quantize_mx(
                out=y_codes[:, u0:u1, :].rearrange("p u w -> p (u w)").bitcast(E4M3X4),
                scales=y_scales[:, u0:u1, :].rearrange("p u w -> p (u w)"),
                in_=y_grouped[:, u0:u1, :].rearrange("p u c -> p (u c)"),
            )

        def mx_pass(dst, u, t, cols, start, stop):
            w_cols = slice(t * P, (t + 1) * P)
            j = group_of(u)
            nc.tensor.matmul_mx(
                out=dst,
                lhsT=w_codes[:, j, w_cols].bitcast(E5M2X4),
                lhsT_scale=w_scales[:, j, w_cols],
                rhs=y_codes[:, u, cols].bitcast(E4M3X4),
                rhs_scale=y_scales[:, u, cols],
                start=start,
                stop=stop,
            )

        def fill(slot, name, u, q):
            zb = bank(slot, name)
            z_banks[u, q] = zb
            for s in range(2):
                mx_pass(zb[:, s * HW : (s + 1) * HW], u, 2 * q + s, slice(0, HW), True, True)

        def product(u, q):
            fill(KEPT_BANKS[u % 2][q // 2] if q % 2 else STAT_BANK, "z_%d_%d" % (u, q), u, q)

        def product_again(u, q):
            fill(AGAIN_BANK, "zz_%d_%d" % (u, q), u, q)

        def sum_passes(u, t0, t1):
            for t in range(t0, t1):
                mx_pass(total[:, 0:HW], u, t, slice(0, HW), t == 0, t == TILES - 1)

        def reduce_sum(u):
            nc.vector.tensor_reduce(out=sums[:, u, PAIRS : PAIRS + 1], in_=total[:, 0:HW], axis=mybir.AxisListType.X, op=ALU.add)

        def sum_squares(u, q):
            nc.scalar.activation(out=squares[:, q, :], in_=z_banks[u, q][:], func=ACT.Square, accum_out=sums[:, u, q : q + 1])

        def averages(row, c0, c1):
            return small[:, STAT_W * row + c0 : STAT_W * row + c1]

        def average_sums(u):
            nc.tensor.matmul(averages(u, 0, PAIRS + 1), lhsT=average[:], rhs=sums[:, u, 0 : PAIRS + 1], start=True, stop=True)

        def take_mean(u):
            mean = averages(u, PAIRS, PAIRS + 1)
            nc.scalar.activation(out=mean_sq[:, u : u + 1], in_=mean, func=ACT.Square, scale=0.5)
            nc.scalar.activation(out=neg_mean[:, u : u + 1], in_=mean, func=ACT.Copy, scale=-1.0)

        def take_variance(u):
            nc.scalar.activation(
                out=terms[:, u, 0:PAIRS], in_=averages(u, 0, PAIRS), func=ACT.Identity,
                scale=-1.0, bias=mean_sq[:, u : u + 1], accum_out=neg_variance[:, u, 0:1],
            )

        def take_std(u):
            nc.scalar.activation(out=std[:, u, 0:1], in_=neg_variance[:, u, 0:1], func=ACT.Sqrt, scale=-1.0, bias=EPS)

        def make_rstd(u):
            nc.vector.reciprocal(out=rstd[:, u, 0:1], in_=std[:, u, 0:1])

        def make_factors(u):
            j = group_of(u)
            nc.scalar.activation(out=factors[:, j, 1 + image_of(u), :], in_=factors[:, j, 0, :], func=ACT.Copy, scale=neg_mean[:, u : u + 1])

        def make_affine(u):
            j, step = group_of(u), 1 + image_of(u)
            nc.vector.scalar_tensor_tensor(
                out=affine[:, u, :, :], in0=factors[:, j, 0 : step + 1 : step, :], scalar=rstd[:, u, 0:1],
                in1=small[:, ADD_COL + 2 * TILES * j : ADD_COL + 2 * TILES * (j + 1)].rearrange("p (r t) -> p r t", r=2), op0=ALU.mult, op1=ALU.add,
            )

        def scale_and_add(u, t):
            cols = slice(t * HW, (t + 1) * HW)
            s = t % 2
            nc.vector.scalar_tensor_tensor(
                out=o_sb[:, u, cols], in0=z_banks[u, t // 2][:, s * HW : (s + 1) * HW], scalar=affine[:, u, 0, t : t + 1],
                in1=x_sb[:, u, cols], op0=ALU.mult, op1=ALU.add,
            )

        def add_shift(u, t):
            cols = slice(t * HW, (t + 1) * HW)
            nc.gpsimd.tensor_scalar(
                out=o_sb[:, u, cols], in0=o_sb[:, u, cols], scalar1=1.0, scalar2=affine[:, u, 1, t : t + 1], op0=ALU.mult, op1=ALU.add
            )

        def add_shift_scalar(u, t):
            cols = slice(t * HW, (t + 1) * HW)
            nc.scalar.activation(out=o_sb[:, u, cols], in_=o_sb[:, u, cols], func=ACT.Identity, bias=affine[:, u, 1, t : t + 1])

        def add_shift_vector(u, t):
            cols = slice(t * HW, (t + 1) * HW)
            nc.vector.tensor_scalar(out=o_sb[:, u, cols], in0=o_sb[:, u, cols], scalar1=affine[:, u, 1, t : t + 1], scalar2=None, op0=ALU.add)

        def place_addends():
            nc.tensor.matmul(
                small[:, ADD_COL : ADD_COL + 2 * G * TILES], lhsT=ident[:], rhs=addends[:].rearrange("p j r t -> p (j r t)"), start=True, stop=True
            )

        def store(u, t0, t1):
            cols = slice(t0 * HW, t1 * HW)
            nc.sync.dma_start(out=out_hbm[image_of(u), group_of(u), :, cols], in_=o_sb[:, u, cols])

        make_identity(nc, ident[:])
        nc.gpsimd.memset(average[:], 1.0 / COUNT)
        nc.gpsimd.memset(addends[:, :, 0, :], 0.0)
        load_w(0, 0, 1)
        load_y(0)
        load_w(0, 1, 2)
        load_w(0, 2, 3)
        load_y(1)
        load_w(0, 3, 4)
        load_w(1, 0, 1)
        nc.sync.dma_start(out=gamma_raw[:], in_=gamma.rearrange("(j p t) -> p j t", j=G, t=TILES))
        nc.sync.dma_start(out=beta_raw[:], in_=beta.rearrange("(j p t) -> p j t", j=G, t=TILES))
        load_y(2)
        load_y(3)
        load_w(1, 1, 2)
        load_w(1, 2, 3)
        load_y(4)
        load_w(1, 3, 4)
        load_y(5)
        for u in range(UNITS):
            load_x(u)

        ones = sb.tile([P, HW], F32)
        root = sb.tile([P, STAT_W], F32)
        nc.vector.memset(ones[:], 1.0)
        nc.scalar.activation(out=root[:, 0:1], in_=ones[:, 0:1], func=ACT.Sqrt)
        nc.tensor.matmul(total[:, 0:HW], lhsT=ones[:, 0:P], rhs=ones[:], start=True, stop=True)
        nc.tensor.matmul(total[:, 0:HW], lhsT=ones[:, 0:P], rhs=ones[:], start=True, stop=True)
        transpose_w(0, 0, 2)
        nc.tensor.matmul(total[:, 0:HW], lhsT=ones[:, 0:P], rhs=ones[:], start=True, stop=True)
        copy_w(0, 0, False)
        interleave_y(0, 1)
        transpose_w(0, 1, 3)
        transpose_w(0, 2, 5)
        nc.tensor.matmul(total[:, 0:HW], lhsT=ones[:, 0:P], rhs=ones[:], start=True, stop=True)
        copy_w(0, 1, False)
        copy_w(0, 2, False)
        quantize_w(0, 0, 1)
        quantize_y(0, 1)
        product(0, 0)
        sum_passes(0, 0, 2)
        sum_squares(0, 0)
        interleave_y(1, 2)
        quantize_w(0, 1, 2)
        quantize_y(1, 2)
        quantize_w(0, 2, 3)
        transpose_w(0, 3, 1)
        transpose_w(1, 0, 2)
        copy_w(0, 3, False)
        nc.scalar.activation(out=factors[:, :, 0, :], in_=gamma_raw[:], func=ACT.Copy)
        nc.scalar.activation(out=addends[:, :, 1, :], in_=beta_raw[:], func=ACT.Copy)
        product(0, 1)
        sum_passes(0, 2, 4)
        sum_squares(0, 1)
        product(0, 2)
        sum_passes(0, 4, 6)
        sum_squares(0, 2)
        copy_w(1, 0, True)
        quantize_w(0, 3, 4)
        quantize_w(1, 0, 1)
        interleave_y(2, 4)
        product(0, 3)
        sum_passes(0, 6, 8)
        sum_squares(0, 3)
        reduce_sum(0)
        quantize_y(2, 4)
        product(1, 0)
        transpose_w(1, 1, 3)
        place_addends()
        average_sums(0)
        sum_squares(1, 0)
        take_mean(0)
        copy_w(1, 1, False)
        take_variance(0)
        make_factors(0)
        take_std(0)
        product(1, 2)
        sum_squares(1, 2)
        sum_passes(1, 0, 3)
        transpose_w(1, 2, 5)
        transpose_w(1, 3, 2)
        interleave_y(4, 6)
        copy_w(1, 2, True)
        copy_w(1, 3, False)
        product(1, 3)
        sum_squares(1, 3)
        sum_passes(1, 3, 8)
        product(1, 1)
        product_again(0, 0)
        make_rstd(0)
        quantize_y(4, 6)
        make_affine(0)
        reduce_sum(1)
        quantize_w(1, 1, 2)
        product(2, 0)

        for u in range(UNITS):
            n1, n2, n3 = u + 1, u + 2, u + 3
            last = n1 == UNITS
            if last:
                for i, t in enumerate((2, 3, 6, 7, 4, 5, 0, 1)):
                    scale_and_add(u, t)
                    if i in (0, 3):
                        add_shift(u, t)
                    elif i < 6:
                        add_shift_scalar(u, t)
                    if i % 2 and i < 6:
                        store(u, t - 1, t + 1)
                for t in (0, 1):
                    add_shift_vector(u, t)
                    store(u, t, t + 1)
                break
            sum_squares(n1, 1 if u == 0 else 3)
            if n2 < UNITS:
                sum_passes(n2, 0, 3)
                sum_squares(n2, 0)
            average_sums(n1)
            take_mean(n1)
            scale_and_add(u, 0)
            add_shift(u, 0)
            scale_and_add(u, 1)
            add_shift_scalar(u, 1)
            take_variance(n1)
            store(u, 0, 2)
            if n2 < UNITS:
                sum_passes(n2, 3, 6)
                product(n2, 2)
            product_again(u, 2)
            scale_and_add(u, 2)
            add_shift(u, 2)
            scale_and_add(u, 3)
            add_shift(u, 3)
            store(u, 2, 4)
            if n2 < UNITS:
                sum_squares(n2, 2)
            take_std(n1)
            make_factors(n1)
            if n2 < UNITS:
                product(n2, 1)
                sum_squares(n2, 1)
                sum_passes(n2, 6, 8)
            scale_and_add(u, 6)
            if n2 < UNITS:
                add_shift(u, 6)
            else:
                add_shift_scalar(u, 6)
            scale_and_add(u, 7)
            if n2 < UNITS:
                add_shift(u, 7)
                product(n2, 3)
            if n3 < UNITS:
                product(n3, 0)
            scale_and_add(u, 4)
            if n2 == UNITS:
                make_rstd(n1)
            scale_and_add(u, 5)
            product_again(n1, 0)
            if n2 < UNITS:
                make_rstd(n1)
                reduce_sum(n2)
                make_affine(n1)
                if u == 0:
                    quantize_w(1, 2, 4)
                for t in (4, 5):
                    add_shift_vector(u, t)
                store(u, 4, TILES)
            else:
                add_shift_scalar(u, 7)
                store(u, 6, 8)
                make_affine(n1)
                add_shift_scalar(u, 4)
                add_shift_scalar(u, 5)
                store(u, 4, 6)
